import numpy as np
import ml_dtypes


def mxq(x, axis, fmt="e4m3"):
    dtype, down = {"e4m3": (ml_dtypes.float8_e4m3fn, 7), "e5m2": (ml_dtypes.float8_e5m2, 14)}[fmt]
    v = np.moveaxis(np.asarray(x, np.float32).astype(ml_dtypes.bfloat16).astype(np.float64), axis, -1)
    blocks = v.reshape(v.shape[:-1] + (-1, 32))
    amax = np.abs(blocks).max(-1, keepdims=True)
    byte = np.maximum(np.where(amax > 0, np.frexp(amax)[1] - 1 + 127, 0) - down, 1)
    scale = np.exp2(byte - 127.0)
    codes = (blocks / scale).astype(np.float32).astype(dtype).astype(np.float64)
    return np.moveaxis((codes * scale).reshape(v.shape), -1, axis)


WIDE = False


def mx_kscale(k):
    if not WIDE:
        return np.ones(k)
    levels = np.array([10, -10, 5, -5, 0])
    a = np.random.permutation(np.resize(levels, k // 512 * 4)).reshape(k // 512, 4)
    idx = np.arange(k)
    return np.exp2(a[idx // 512, idx % 128 // 32])


BF16 = ml_dtypes.bfloat16


def bf(x):
    return np.asarray(x, np.float32).astype(BF16)


def f64(x):
    return np.asarray(x).astype(np.float64)


B, N, D, K, R, G = 2, 8192, 512, 256, 8, 16
EPS = 1e-8


def norm(v):
    return np.sqrt((v * v).sum(-1, keepdims=True))


def mix(z, p):
    return sum(z[..., r:r + 1] * p[:, None, r, :] for r in range(R)) / np.sqrt(R)


def setup_inputs():
    p = np.random.standard_normal((B, R, D))
    x = 3.0 * (mix(np.random.standard_normal((B, N, R)), p) + 0.5 * np.random.standard_normal((B, N, D)))
    centers = mix(np.random.standard_normal((B, K, R)), p) + 0.5 * np.random.standard_normal((B, K, D))
    g = mx_kscale(N).max()
    if g > 1.0:
        z = np.arange(D) % 2 == 1
        big = (np.arange(N) // (N // G)) % 4 == 1
        centers[:, :, z] = 0.0
        w = 3.0 * np.repeat(np.random.standard_normal((B, N // 2, D)), 2, axis=1)
        w[:, 1::2] *= -1.0
        x[:, big] = (w * np.where(z, np.exp2(np.round(1.8 * np.log2(g))), 1.0 / g))[:, big]
    return {"x": bf(x), "centers": bf(centers)}


def reference(x, centers):
    x, centers = f64(x), f64(centers)
    tn = x / (norm(x) + EPS)
    cn = centers / (norm(centers) + EPS)
    tn2 = tn / np.maximum(norm(tn), EPS)
    cn2 = cn / np.maximum(norm(cn), EPS)
    cos_sim = mxq(tn2, 2, "e4m3") @ mxq(cn2, 2, "e4m3").transpose(0, 2, 1)
    dist = 1.0 - cos_sim
    e = np.exp(-dist - (-dist).max(-1, keepdims=True))
    prob = e / e.sum(-1, keepdims=True)
    num = mxq(prob, 1, "e4m3").transpose(0, 2, 1) @ mxq(x, 1, "e4m3")
    den = prob.sum(1)[..., None] + EPS
    return num / den

@@ -1,0 +1,294 @@
+from contextlib import ExitStack
+
+import concourse.mybir as mybir
+from concourse.masks import make_identity
+
+FP8X4 = mybir.dt.float8_e4m3fn_x4
+BF16 = mybir.dt.bfloat16
+F32 = mybir.dt.float32
+U32 = mybir.dt.uint32
+U8 = mybir.dt.uint8
+ALU = mybir.AluOpType
+ACT = mybir.ActivationFunctionType
+AX = mybir.AxisListType
+
+P = 128
+PACK = 4
+B, N, D, K = 2, 8192, 512, 256
+BLOCK = P * PACK
+NBLK = N // BLOCK
+NB = B * NBLK
+EPS = 1e-8
+FLOPS = 2 * 2 * B * N * D * K
+
+VECTOR_COPY_EVERY = 8
+CENTRES = -1
+
+
+def tile_token_merging_t_kernel(tc, x, centers, out):
+    nc = tc.nc
+    with ExitStack() as ctx:
+        keep = ctx.enter_context(tc.tile_pool(name="keep", bufs=1))
+        work = ctx.enter_context(tc.tile_pool(name="work", bufs=3))
+        turn_pool = ctx.enter_context(tc.psum_pool(name="turn", bufs=3))
+        cos_pool = ctx.enter_context(tc.psum_pool(name="cosp", bufs=2))
+        acc_pool = ctx.enter_context(tc.psum_pool(name="acc", bufs=1))
+        ctx.enter_context(tc.manual_schedule())
+
+        ident = keep.tile([P, P], BF16)
+        make_identity(nc, ident[:])
+        half = keep.tile([P, PACK], F32)
+        nc.vector.memset(half[:], 0.5)
+
+        c_rows = keep.tile([P, PACK, D], BF16)
+        nc.sync.dma_start(out=c_rows[:], in_=centers.rearrange("b (a p) d -> p (b a) d", p=P))
+        x_all = keep.tile([P, NB, PACK, D], BF16)
+        x_blocks = x.rearrange("b (g p j) d -> (b g) p j d", p=P, j=PACK)
+        for i in range(NB):
+            nc.sync.dma_start(out=x_all[:, i, :, :], in_=x_blocks[i])
+
+        c_codes = keep.tile([P, B * K], U32, align_bytes=64)
+        c_scales = keep.tile([P, B * K], U8, align_bytes=64)
+        den_ps = acc_pool.tile([P, B, 2, NBLK], F32)
+
+        st = {}
+
+        def rows_of(i):
+            return c_rows[:] if i == CENTRES else x_all[:, i, :, :]
+
+        def sum_squares(i):
+            sumsq = work.tile([P, PACK], F32)
+            for j in range(PACK):
+                junk = work.tile([P, D], BF16)
+                nc.scalar.activation(
+                    out=junk[:],
+                    in_=rows_of(i)[:, j, :],
+                    func=ACT.Square,
+                    accum_out=sumsq[:, j : j + 1],
+                )
+            st[("sumsq", i)] = sumsq
+
+        def root(i):
+            norm = work.tile([P, PACK], F32)
+            nc.gpsimd.tensor_tensor(out=norm[:], in0=st[("sumsq", i)][:], in1=half[:], op=ALU.pow)
+            st[("norm", i)] = norm
+
+        def scale_rows(i):
+            norm = st[("norm", i)]
+            floor = work.tile([P, PACK], F32)
+            nc.vector.tensor_scalar(
+                out=floor[:], in0=norm[:], scalar1=EPS, scalar2=EPS * EPS, op0=ALU.mult, op1=ALU.add
+            )
+            divisor = work.tile([P, PACK], F32)
+            nc.vector.tensor_tensor(out=divisor[:], in0=floor[:], in1=norm[:], op=ALU.max)
+            inv = work.tile([P, PACK], F32)
+            nc.vector.reciprocal(out=inv[:], in_=divisor[:])
+            unit = work.tile([P, PACK, D], BF16)
+            for j in range(PACK):
+                nc.vector.tensor_scalar(
+                    out=unit[:, j, :],
+                    in0=rows_of(i)[:, j, :],
+                    scalar1=inv[:, j : j + 1],
+                    scalar2=None,
+                    op0=ALU.mult,
+                )
+            st[("unit", i)] = unit
+
+        def turn(i):
+            unit = st[("unit", i)]
+            for h in range(2):
+                turned = turn_pool.tile([P, 2, PACK, P], BF16)
+                for a in range(2):
+                    for t in range(PACK):
+                        nc.tensor.transpose(
+                            turned[:, a, t, :], unit[:, 2 * h + a, t * P : (t + 1) * P], ident[:]
+                        )
+                st[("turned", i, h)] = turned
+
+        def regroup_turned(i):
+            grouped = work.tile([P, PACK, P, PACK], BF16, align_bytes=64)
+            for h in range(2):
+                src = st[("turned", i, h)][:].rearrange("p a t c -> p a c t")
+                dst = grouped[:, 2 * h : 2 * h + 2, :, :]
+                if (2 * i + h) % VECTOR_COPY_EVERY == 0:
+                    nc.vector.tensor_copy(out=dst, in_=src)
+                else:
+                    nc.scalar.copy(out=dst, in_=src)
+            st[("grouped", i)] = grouped
+
+        def quantise_unit(i):
+            if i == CENTRES:
+                codes, scales = c_codes, c_scales
+            else:
+                t_codes = work.tile([P, BLOCK], U32, align_bytes=64)
+                t_scales = work.tile([P, BLOCK], U8, align_bytes=64)
+                codes, scales = t_codes, t_scales
+            nc.vector.quantize_mx(
+                out=codes[:].bitcast(FP8X4),
+                scales=scales[:],
+                in_=st[("grouped", i)][:].rearrange("p j c t -> p (j c t)"),
+            )
+            st[("t", i)] = (codes, scales)
+
+        def regroup_x(i):
+            x_grouped = work.tile([P, D, PACK], BF16, align_bytes=64)
+            nc.vector.tensor_copy(
+                out=x_grouped[:].rearrange("p (c i) t -> p c t i", i=4),
+                in_=rows_of(i).rearrange("p t (c i) -> p c t i", i=4),
+            )
+            st[("xg", i)] = x_grouped
+
+        def quantise_x(i):
+            x_codes = work.tile([P, D], U32, align_bytes=64)
+            x_scales = work.tile([P, D], U8, align_bytes=64)
+            nc.vector.quantize_mx(
+                out=x_codes[:].bitcast(FP8X4),
+                scales=x_scales[:],
+                in_=st[("xg", i)][:].rearrange("p c t -> p (c t)"),
+            )
+            st[("x", i)] = (x_codes, x_scales)
+
+        def cosines(i):
+            b = i // NBLK
+            codes, scales = st[("t", i)]
+            for h in range(2):
+                cos = cos_pool.tile([P, 2, K], F32)
+                for a in range(2):
+                    j = 2 * h + a
+                    nc.tensor.matmul_mx(
+                        out=cos[:, a, :],
+                        lhsT=codes[:, j * P : (j + 1) * P].bitcast(FP8X4),
+                        lhsT_scale=scales[:, j * P : (j + 1) * P],
+                        rhs=c_codes[:, b * K : (b + 1) * K].bitcast(FP8X4),
+                        rhs_scale=c_scales[:, b * K : (b + 1) * K],
+                        start=True,
+                        stop=True,
+                    )
+                st[("cos", i, h)] = cos
+
+        def row_max(i):
+            negmax = work.tile([P, PACK], F32)
+            for h in range(2):
+                nc.vector.tensor_reduce(
+                    out=negmax[:, 2 * h : 2 * h + 2],
+                    in_=st[("cos", i, h)][:],
+                    axis=AX.X,
+                    op=ALU.max,
+                    negate=True,
+                )
+            st[("negmax", i)] = negmax
+
+        def exponentials(i):
+            negmax = st[("negmax", i)]
+            esum = work.tile([P, PACK], F32)
+            e = work.tile([P, PACK, K], F32)
+            for j in range(PACK):
+                nc.scalar.activation(
+                    out=e[:, j, :],
+                    in_=st[("cos", i, j // 2)][:, j % 2, :],
+                    func=ACT.Exp,
+                    bias=negmax[:, j : j + 1],
+                    scale=1.0,
+                    accum_out=esum[:, j : j + 1],
+                )
+            st[("e", i)] = (e, esum)
+
+        def probabilities(i):
+            e, esum = st[("e", i)]
+            rsum = work.tile([P, PACK], F32)
+            nc.vector.reciprocal(out=rsum[:], in_=esum[:])
+            p_grouped = work.tile([P, K, PACK], BF16, align_bytes=64)
+            nc.vector.tensor_tensor(
+                out=p_grouped[:],
+                in0=e[:].rearrange("p j k -> p k j"),
+                in1=rsum[:].unsqueeze(1).to_broadcast([P, K, PACK]),
+                op=ALU.mult,
+            )
+            p_codes = work.tile([P, K], U32, align_bytes=64)
+            p_scales = work.tile([P, K], U8, align_bytes=64)
+            nc.vector.quantize_mx(
+                out=p_codes[:].bitcast(FP8X4),
+                scales=p_scales[:],
+                in_=p_grouped[:].rearrange("p k j -> p (k j)"),
+            )
+            st[("p", i)] = (p_codes, p_scales, rsum)
+
+        def accumulate(i):
+            b, g = i // NBLK, i % NBLK
+            if g == 0:
+                num0 = acc_pool.tile([P, D], F32)
+                num1 = acc_pool.tile([P, D], F32)
+                st[("num", b)] = [num0, num1]
+            num = st[("num", b)]
+            p_codes, p_scales, rsum = st[("p", i)]
+            x_codes, x_scales = st[("x", i)]
+            e = st[("e", i)][0]
+            for h in range(2):
+                nc.tensor.matmul_mx(
+                    out=num[h][:],
+                    lhsT=p_codes[:, h * P : (h + 1) * P].bitcast(FP8X4),
+                    lhsT_scale=p_scales[:, h * P : (h + 1) * P],
+                    rhs=x_codes[:].bitcast(FP8X4),
+                    rhs_scale=x_scales[:],
+                    start=(g == 0),
+                    stop=(g == NBLK - 1),
+                )
+            for h in range(2):
+                for j in range(PACK):
+                    nc.tensor.matmul(
+                        out=den_ps[:, b, h, g : g + 1],
+                        lhsT=e[:, j, h * P : (h + 1) * P],
+                        rhs=rsum[:, j : j + 1],
+                        start=(j == 0),
+                        stop=(j == PACK - 1),
+                    )
+
+        def finish(b):
+            den = work.tile([P, 2], F32)
+            nc.vector.tensor_reduce(out=den[:], in_=den_ps[:, b, :, :], axis=AX.X, op=ALU.add)
+            den_eps = work.tile([P, 2], F32)
+            nc.vector.tensor_scalar_add(out=den_eps[:], in0=den[:], scalar1=EPS)
+            rden = work.tile([P, 2], F32)
+            nc.vector.reciprocal(out=rden[:], in_=den_eps[:])
+            for h in range(2):
+                merged = work.tile([P, D], F32)
+                nc.scalar.activation(
+                    out=merged[:], in_=st[("num", b)][h][:], func=ACT.Copy, scale=rden[:, h : h + 1]
+                )
+                nc.sync.dma_start(out=out[b, h * P : (h + 1) * P, :], in_=merged[:])
+
+        def prep(i):
+            return CENTRES <= i < NB
+
+        def real(i):
+            return 0 <= i < NB
+
+        for it in range(CENTRES, NB + 3):
+            if prep(it - 2):
+                quantise_unit(it - 2)
+            if real(it - 2):
+                cosines(it - 2)
+            if prep(it):
+                sum_squares(it)
+            if real(it - 2):
+                regroup_x(it - 2)
+            if prep(it - 1):
+                turn(it - 1)
+            if prep(it):
+                root(it)
+            if real(it - 2):
+                row_max(it - 2)
+            if prep(it - 1):
+                regroup_turned(it - 1)
+            if real(it - 4) and (it - 4) % NBLK == NBLK - 1:
+                finish((it - 4) // NBLK)
+            if real(it - 3):
+                probabilities(it - 3)
+            if real(it - 2):
+                quantise_x(it - 2)
+                exponentials(it - 2)
+            if real(it - 3):
+                accumulate(it - 3)
+            if prep(it):
+                scale_rows(it)
+        finish(B - 1)

@@ -21,7 +21,6 @@ NB = B * NBLK
 EPS = 1e-8
 FLOPS = 2 * 2 * B * N * D * K
 
-VECTOR_COPY_EVERY = 8
 CENTRES = -1
 
 
@@ -30,15 +29,17 @@ def tile_token_merging_t_kernel(tc, x, centers, out):
     with ExitStack() as ctx:
         keep = ctx.enter_context(tc.tile_pool(name="keep", bufs=1))
         work = ctx.enter_context(tc.tile_pool(name="work", bufs=3))
-        turn_pool = ctx.enter_context(tc.psum_pool(name="turn", bufs=3))
+        turn_pool = ctx.enter_context(tc.psum_pool(name="turn", bufs=2))
         cos_pool = ctx.enter_context(tc.psum_pool(name="cosp", bufs=2))
         acc_pool = ctx.enter_context(tc.psum_pool(name="acc", bufs=1))
         ctx.enter_context(tc.manual_schedule())
 
         ident = keep.tile([P, P], BF16)
         make_identity(nc, ident[:])
-        half = keep.tile([P, PACK], F32)
-        nc.vector.memset(half[:], 0.5)
+        ident_f = keep.tile([P, P], F32)
+        make_identity(nc, ident_f[:])
+        neg_half = keep.tile([P, PACK], F32)
+        nc.vector.memset(neg_half[:], -0.5)
 
         c_rows = keep.tile([P, PACK, D], BF16)
         nc.sync.dma_start(out=c_rows[:], in_=centers.rearrange("b (a p) d -> p (b a) d", p=P))
@@ -49,7 +50,6 @@ def tile_token_merging_t_kernel(tc, x, centers, out):
 
         c_codes = keep.tile([P, B * K], U32, align_bytes=64)
         c_scales = keep.tile([P, B * K], U8, align_bytes=64)
-        den_ps = acc_pool.tile([P, B, 2, NBLK], F32)
 
         st = {}
 
@@ -68,21 +68,15 @@ def tile_token_merging_t_kernel(tc, x, centers, out):
                 )
             st[("sumsq", i)] = sumsq
 
-        def root(i):
-            norm = work.tile([P, PACK], F32)
-            nc.gpsimd.tensor_tensor(out=norm[:], in0=st[("sumsq", i)][:], in1=half[:], op=ALU.pow)
-            st[("norm", i)] = norm
+        def inverse_norm(i):
+            clamped = work.tile([P, PACK], F32)
+            nc.gpsimd.tensor_scalar_max(out=clamped[:], in0=st[("sumsq", i)][:], scalar1=EPS**4)
+            inv = work.tile([P, PACK], F32)
+            nc.gpsimd.tensor_tensor(out=inv[:], in0=clamped[:], in1=neg_half[:], op=ALU.pow)
+            st[("inv", i)] = inv
 
         def scale_rows(i):
-            norm = st[("norm", i)]
-            floor = work.tile([P, PACK], F32)
-            nc.vector.tensor_scalar(
-                out=floor[:], in0=norm[:], scalar1=EPS, scalar2=EPS * EPS, op0=ALU.mult, op1=ALU.add
-            )
-            divisor = work.tile([P, PACK], F32)
-            nc.vector.tensor_tensor(out=divisor[:], in0=floor[:], in1=norm[:], op=ALU.max)
-            inv = work.tile([P, PACK], F32)
-            nc.vector.reciprocal(out=inv[:], in_=divisor[:])
+            inv = st[("inv", i)]
             unit = work.tile([P, PACK, D], BF16)
             for j in range(PACK):
                 nc.vector.tensor_scalar(
@@ -108,12 +102,10 @@ def tile_token_merging_t_kernel(tc, x, centers, out):
         def regroup_turned(i):
             grouped = work.tile([P, PACK, P, PACK], BF16, align_bytes=64)
             for h in range(2):
-                src = st[("turned", i, h)][:].rearrange("p a t c -> p a c t")
-                dst = grouped[:, 2 * h : 2 * h + 2, :, :]
-                if (2 * i + h) % VECTOR_COPY_EVERY == 0:
-                    nc.vector.tensor_copy(out=dst, in_=src)
-                else:
-                    nc.scalar.copy(out=dst, in_=src)
+                nc.scalar.copy(
+                    out=grouped[:, 2 * h : 2 * h + 2, :, :],
+                    in_=st[("turned", i, h)][:].rearrange("p a t c -> p a c t"),
+                )
             st[("grouped", i)] = grouped
 
         def quantise_unit(i):
@@ -197,13 +189,17 @@ def tile_token_merging_t_kernel(tc, x, centers, out):
             e, esum = st[("e", i)]
             rsum = work.tile([P, PACK], F32)
             nc.vector.reciprocal(out=rsum[:], in_=esum[:])
+            prob = work.tile([P, PACK, K], F32)
+            for j in range(PACK):
+                nc.vector.tensor_scalar(
+                    out=prob[:, j, :],
+                    in0=e[:, j, :],
+                    scalar1=rsum[:, j : j + 1],
+                    scalar2=None,
+                    op0=ALU.mult,
+                )
             p_grouped = work.tile([P, K, PACK], BF16, align_bytes=64)
-            nc.vector.tensor_tensor(
-                out=p_grouped[:],
-                in0=e[:].rearrange("p j k -> p k j"),
-                in1=rsum[:].unsqueeze(1).to_broadcast([P, K, PACK]),
-                op=ALU.mult,
-            )
+            nc.vector.tensor_copy(out=p_grouped[:], in_=prob[:].rearrange("p j k -> p k j"))
             p_codes = work.tile([P, K], U32, align_bytes=64)
             p_scales = work.tile([P, K], U8, align_bytes=64)
             nc.vector.quantize_mx(
@@ -211,21 +207,37 @@ def tile_token_merging_t_kernel(tc, x, centers, out):
                 scales=p_scales[:],
                 in_=p_grouped[:].rearrange("p k j -> p (k j)"),
             )
-            st[("p", i)] = (p_codes, p_scales, rsum)
+            st[("p", i)] = (p_codes, p_scales, prob)
 
-        def accumulate(i):
+        def add_probabilities(i):
+            b, g = i // NBLK, i % NBLK
+            if g == 0:
+                sum0 = acc_pool.tile([P, P], F32)
+                sum1 = acc_pool.tile([P, P], F32)
+                st[("sum", b)] = [sum0, sum1]
+            prob = st[("p", i)][2]
+            for h in range(2):
+                for j in range(PACK):
+                    nc.tensor.matmul(
+                        out=st[("sum", b)][h][:],
+                        lhsT=prob[:, j, h * P : (h + 1) * P],
+                        rhs=ident_f[:],
+                        is_transpose=True,
+                        start=(g == 0 and j == 0),
+                        stop=(g == NBLK - 1 and j == PACK - 1),
+                    )
+
+        def merge(i):
             b, g = i // NBLK, i % NBLK
             if g == 0:
                 num0 = acc_pool.tile([P, D], F32)
                 num1 = acc_pool.tile([P, D], F32)
                 st[("num", b)] = [num0, num1]
-            num = st[("num", b)]
-            p_codes, p_scales, rsum = st[("p", i)]
+            p_codes, p_scales = st[("p", i)][0], st[("p", i)][1]
             x_codes, x_scales = st[("x", i)]
-            e = st[("e", i)][0]
             for h in range(2):
                 nc.tensor.matmul_mx(
-                    out=num[h][:],
+                    out=st[("num", b)][h][:],
                     lhsT=p_codes[:, h * P : (h + 1) * P].bitcast(FP8X4),
                     lhsT_scale=p_scales[:, h * P : (h + 1) * P],
                     rhs=x_codes[:].bitcast(FP8X4),
@@ -233,19 +245,13 @@ def tile_token_merging_t_kernel(tc, x, centers, out):
                     start=(g == 0),
                     stop=(g == NBLK - 1),
                 )
-            for h in range(2):
-                for j in range(PACK):
-                    nc.tensor.matmul(
-                        out=den_ps[:, b, h, g : g + 1],
-                        lhsT=e[:, j, h * P : (h + 1) * P],
-                        rhs=rsum[:, j : j + 1],
-                        start=(j == 0),
-                        stop=(j == PACK - 1),
-                    )
 
         def finish(b):
             den = work.tile([P, 2], F32)
-            nc.vector.tensor_reduce(out=den[:], in_=den_ps[:, b, :, :], axis=AX.X, op=ALU.add)
+            for h in range(2):
+                nc.vector.tensor_reduce(
+                    out=den[:, h : h + 1], in_=st[("sum", b)][h][:], axis=AX.X, op=ALU.add
+                )
             den_eps = work.tile([P, 2], F32)
             nc.vector.tensor_scalar_add(out=den_eps[:], in0=den[:], scalar1=EPS)
             rden = work.tile([P, 2], F32)
@@ -263,32 +269,34 @@ def tile_token_merging_t_kernel(tc, x, centers, out):
         def real(i):
             return 0 <= i < NB
 
-        for it in range(CENTRES, NB + 3):
+        for it in range(CENTRES, NB + 5):
+            if real(it - 6) and (it - 6) % NBLK == NBLK - 1:
+                finish((it - 6) // NBLK)
+            if real(it - 4):
+                exponentials(it - 4)
             if prep(it - 2):
-                quantise_unit(it - 2)
-            if real(it - 2):
-                cosines(it - 2)
+                turn(it - 2)
+            if prep(it - 3):
+                quantise_unit(it - 3)
+            if real(it - 4):
+                regroup_x(it - 4)
+            if prep(it - 2):
+                regroup_turned(it - 2)
+            if real(it - 5):
+                add_probabilities(it - 5)
+            if real(it - 4):
+                probabilities(it - 4)
+            if real(it - 3):
+                cosines(it - 3)
+            if real(it - 4):
+                quantise_x(it - 4)
             if prep(it):
                 sum_squares(it)
-            if real(it - 2):
-                regroup_x(it - 2)
+                inverse_norm(it)
             if prep(it - 1):
-                turn(it - 1)
-            if prep(it):
-                root(it)
-            if real(it - 2):
-                row_max(it - 2)
-            if prep(it - 1):
-                regroup_turned(it - 1)
-            if real(it - 4) and (it - 4) % NBLK == NBLK - 1:
-                finish((it - 4) // NBLK)
+                scale_rows(it - 1)
+            if real(it - 5):
+                merge(it - 5)
             if real(it - 3):
-                probabilities(it - 3)
-            if real(it - 2):
-                quantise_x(it - 2)
-                exponentials(it - 2)
-            if real(it - 3):
-                accumulate(it - 3)
-            if prep(it):
-                scale_rows(it)
+                row_max(it - 3)
         finish(B - 1)

@@ -22,13 +22,16 @@ EPS = 1e-8
 FLOPS = 2 * 2 * B * N * D * K
 
 CENTRES = -1
+X_LEAD = 3
+X_BUFS = X_LEAD + 7
 
 
 def tile_token_merging_t_kernel(tc, x, centers, out):
     nc = tc.nc
     with ExitStack() as ctx:
         keep = ctx.enter_context(tc.tile_pool(name="keep", bufs=1))
-        work = ctx.enter_context(tc.tile_pool(name="work", bufs=3))
+        work = ctx.enter_context(tc.tile_pool(name="work", bufs=2))
+        xq_pool = ctx.enter_context(tc.tile_pool(name="xq", bufs=X_BUFS))
         turn_pool = ctx.enter_context(tc.psum_pool(name="turn", bufs=2))
         cos_pool = ctx.enter_context(tc.psum_pool(name="cosp", bufs=2))
         acc_pool = ctx.enter_context(tc.psum_pool(name="acc", bufs=1))
@@ -75,10 +78,13 @@ def tile_token_merging_t_kernel(tc, x, centers, out):
             nc.gpsimd.tensor_tensor(out=inv[:], in0=clamped[:], in1=neg_half[:], op=ALU.pow)
             st[("inv", i)] = inv
 
-        def scale_rows(i):
+        def scale_rows(i, part):
             inv = st[("inv", i)]
-            unit = work.tile([P, PACK, D], BF16)
-            for j in range(PACK):
+            if part == 0:
+                unit = work.tile([P, PACK, D], BF16)
+                st[("unit", i)] = unit
+            unit = st[("unit", i)]
+            for j in (2 * part, 2 * part + 1):
                 nc.vector.tensor_scalar(
                     out=unit[:, j, :],
                     in0=rows_of(i)[:, j, :],
@@ -86,7 +92,6 @@ def tile_token_merging_t_kernel(tc, x, centers, out):
                     scalar2=None,
                     op0=ALU.mult,
                 )
-            st[("unit", i)] = unit
 
         def turn(i):
             unit = st[("unit", i)]
@@ -123,7 +128,7 @@ def tile_token_merging_t_kernel(tc, x, centers, out):
             st[("t", i)] = (codes, scales)
 
         def regroup_x(i):
-            x_grouped = work.tile([P, D, PACK], BF16, align_bytes=64)
+            x_grouped = work.tile([P, D, PACK], BF16, align_bytes=64, bufs=3)
             nc.vector.tensor_copy(
                 out=x_grouped[:].rearrange("p (c i) t -> p c t i", i=4),
                 in_=rows_of(i).rearrange("p t (c i) -> p c t i", i=4),
@@ -131,8 +136,8 @@ def tile_token_merging_t_kernel(tc, x, centers, out):
             st[("xg", i)] = x_grouped
 
         def quantise_x(i):
-            x_codes = work.tile([P, D], U32, align_bytes=64)
-            x_scales = work.tile([P, D], U8, align_bytes=64)
+            x_codes = xq_pool.tile([P, D], U32, align_bytes=64)
+            x_scales = xq_pool.tile([P, D], U8, align_bytes=64)
             nc.vector.quantize_mx(
                 out=x_codes[:].bitcast(FP8X4),
                 scales=x_scales[:],
@@ -185,10 +190,14 @@ def tile_token_merging_t_kernel(tc, x, centers, out):
                 )
             st[("e", i)] = (e, esum)
 
-        def probabilities(i):
-            e, esum = st[("e", i)]
+        def inverse_sums(i):
             rsum = work.tile([P, PACK], F32)
-            nc.vector.reciprocal(out=rsum[:], in_=esum[:])
+            nc.vector.reciprocal(out=rsum[:], in_=st[("e", i)][1][:])
+            st[("rsum", i)] = rsum
+
+        def probabilities(i):
+            e = st[("e", i)][0]
+            rsum = st[("rsum", i)]
             prob = work.tile([P, PACK, K], F32)
             for j in range(PACK):
                 nc.vector.tensor_scalar(
@@ -198,16 +207,24 @@ def tile_token_merging_t_kernel(tc, x, centers, out):
                     scalar2=None,
                     op0=ALU.mult,
                 )
+            st[("prob", i)] = prob
+
+        def regroup_prob(i):
             p_grouped = work.tile([P, K, PACK], BF16, align_bytes=64)
-            nc.vector.tensor_copy(out=p_grouped[:], in_=prob[:].rearrange("p j k -> p k j"))
+            nc.vector.tensor_copy(
+                out=p_grouped[:], in_=st[("prob", i)][:].rearrange("p j k -> p k j")
+            )
+            st[("pg", i)] = p_grouped
+
+        def quantise_prob(i):
             p_codes = work.tile([P, K], U32, align_bytes=64)
             p_scales = work.tile([P, K], U8, align_bytes=64)
             nc.vector.quantize_mx(
                 out=p_codes[:].bitcast(FP8X4),
                 scales=p_scales[:],
-                in_=p_grouped[:].rearrange("p k j -> p (k j)"),
+                in_=st[("pg", i)][:].rearrange("p k j -> p (k j)"),
             )
-            st[("p", i)] = (p_codes, p_scales, prob)
+            st[("p", i)] = (p_codes, p_scales)
 
         def add_probabilities(i):
             b, g = i // NBLK, i % NBLK
@@ -215,7 +232,7 @@ def tile_token_merging_t_kernel(tc, x, centers, out):
                 sum0 = acc_pool.tile([P, P], F32)
                 sum1 = acc_pool.tile([P, P], F32)
                 st[("sum", b)] = [sum0, sum1]
-            prob = st[("p", i)][2]
+            prob = st[("prob", i)]
             for h in range(2):
                 for j in range(PACK):
                     nc.tensor.matmul(
@@ -269,7 +286,9 @@ def tile_token_merging_t_kernel(tc, x, centers, out):
         def real(i):
             return 0 <= i < NB
 
+        early = {-1: [0], 0: [1], 1: [2, 3], 2: [4, 5]}
         for it in range(CENTRES, NB + 5):
+            x_now = early.get(it, [it + X_LEAD] if it + X_LEAD < NB else [])
             if real(it - 6) and (it - 6) % NBLK == NBLK - 1:
                 finish((it - 6) // NBLK)
             if real(it - 4):
@@ -278,23 +297,31 @@ def tile_token_merging_t_kernel(tc, x, centers, out):
                 turn(it - 2)
             if prep(it - 3):
                 quantise_unit(it - 3)
-            if real(it - 4):
-                regroup_x(it - 4)
+            for i in x_now:
+                regroup_x(i)
             if prep(it - 2):
                 regroup_turned(it - 2)
             if real(it - 5):
                 add_probabilities(it - 5)
             if real(it - 4):
+                inverse_sums(it - 4)
+            if prep(it - 1):
+                scale_rows(it - 1, 0)
+            if real(it - 4):
                 probabilities(it - 4)
+            if prep(it - 1):
+                scale_rows(it - 1, 1)
+            if real(it - 4):
+                regroup_prob(it - 4)
             if real(it - 3):
                 cosines(it - 3)
+            for i in x_now:
+                quantise_x(i)
             if real(it - 4):
-                quantise_x(it - 4)
+                quantise_prob(it - 4)
             if prep(it):
                 sum_squares(it)
                 inverse_norm(it)
-            if prep(it - 1):
-                scale_rows(it - 1)
             if real(it - 5):
                 merge(it - 5)
             if real(it - 3):

@@ -22,6 +22,7 @@ EPS = 1e-8
 FLOPS = 2 * 2 * B * N * D * K
 
 CENTRES = -1
+VECTOR_COPY_EVERY = 3
 X_LEAD = 3
 X_BUFS = X_LEAD + 7
 
@@ -107,7 +108,8 @@ def tile_token_merging_t_kernel(tc, x, centers, out):
         def regroup_turned(i):
             grouped = work.tile([P, PACK, P, PACK], BF16, align_bytes=64)
             for h in range(2):
-                nc.scalar.copy(
+                copier = nc.vector.tensor_copy if (2 * i + h) % VECTOR_COPY_EVERY == 1 else nc.scalar.copy
+                copier(
                     out=grouped[:, 2 * h : 2 * h + 2, :, :],
                     in_=st[("turned", i, h)][:].rearrange("p a t c -> p a c t"),
                 )

@@ -22,7 +22,8 @@ EPS = 1e-8
 FLOPS = 2 * 2 * B * N * D * K
 
 CENTRES = -1
-VECTOR_COPY_EVERY = 3
+VECTOR_COPY_EVERY = 6
+VECTOR_COPY_LATE = 26
 X_LEAD = 3
 X_BUFS = X_LEAD + 7
 
@@ -46,7 +47,9 @@ def tile_token_merging_t_kernel(tc, x, centers, out):
         nc.vector.memset(neg_half[:], -0.5)
 
         c_rows = keep.tile([P, PACK, D], BF16)
-        nc.sync.dma_start(out=c_rows[:], in_=centers.rearrange("b (a p) d -> p (b a) d", p=P))
+        c_view = centers.rearrange("b (a p) d -> p (b a) d", p=P)
+        for j in range(PACK):
+            nc.sync.dma_start(out=c_rows[:, j, :], in_=c_view[:, j, :])
         x_all = keep.tile([P, NB, PACK, D], BF16)
         x_blocks = x.rearrange("b (g p j) d -> (b g) p j d", p=P, j=PACK)
         for i in range(NB):
@@ -108,7 +111,11 @@ def tile_token_merging_t_kernel(tc, x, centers, out):
         def regroup_turned(i):
             grouped = work.tile([P, PACK, P, PACK], BF16, align_bytes=64)
             for h in range(2):
-                copier = nc.vector.tensor_copy if (2 * i + h) % VECTOR_COPY_EVERY == 1 else nc.scalar.copy
+                if i >= VECTOR_COPY_LATE:
+                    on_vector = h == 1
+                else:
+                    on_vector = (2 * i + h) % VECTOR_COPY_EVERY == 1
+                copier = nc.vector.tensor_copy if on_vector else nc.scalar.copy
                 copier(
                     out=grouped[:, 2 * h : 2 * h + 2, :, :],
                     in_=st[("turned", i, h)][:].rearrange("p a t c -> p a c t"),
@@ -277,9 +284,18 @@ def tile_token_merging_t_kernel(tc, x, centers, out):
             nc.vector.reciprocal(out=rden[:], in_=den_eps[:])
             for h in range(2):
                 merged = work.tile([P, D], F32)
-                nc.scalar.activation(
-                    out=merged[:], in_=st[("num", b)][h][:], func=ACT.Copy, scale=rden[:, h : h + 1]
-                )
+                if h == 0:
+                    nc.scalar.activation(
+                        out=merged[:], in_=st[("num", b)][h][:], func=ACT.Copy, scale=rden[:, h : h + 1]
+                    )
+                else:
+                    nc.vector.tensor_scalar(
+                        out=merged[:],
+                        in0=st[("num", b)][h][:],
+                        scalar1=rden[:, h : h + 1],
+                        scalar2=None,
+                        op0=ALU.mult,
+                    )
                 nc.sync.dma_start(out=out[b, h * P : (h + 1) * P, :], in_=merged[:])
 
         def prep(i):

@@ -25,7 +25,7 @@ CENTRES = -1
 VECTOR_COPY_EVERY = 6
 VECTOR_COPY_LATE = 26
 X_LEAD = 3
-X_BUFS = X_LEAD + 7
+X_BUFS = X_LEAD + 9
 
 
 def tile_token_merging_t_kernel(tc, x, centers, out):
@@ -33,6 +33,7 @@ def tile_token_merging_t_kernel(tc, x, centers, out):
     with ExitStack() as ctx:
         keep = ctx.enter_context(tc.tile_pool(name="keep", bufs=1))
         work = ctx.enter_context(tc.tile_pool(name="work", bufs=2))
+        norms = ctx.enter_context(tc.tile_pool(name="norms", bufs=4))
         xq_pool = ctx.enter_context(tc.tile_pool(name="xq", bufs=X_BUFS))
         turn_pool = ctx.enter_context(tc.psum_pool(name="turn", bufs=2))
         cos_pool = ctx.enter_context(tc.psum_pool(name="cosp", bufs=2))
@@ -43,7 +44,7 @@ def tile_token_merging_t_kernel(tc, x, centers, out):
         make_identity(nc, ident[:])
         ident_f = keep.tile([P, P], F32)
         make_identity(nc, ident_f[:])
-        neg_half = keep.tile([P, PACK], F32)
+        neg_half = keep.tile([P, 2 * PACK], F32)
         nc.vector.memset(neg_half[:], -0.5)
 
         c_rows = keep.tile([P, PACK, D], BF16)
@@ -63,27 +64,38 @@ def tile_token_merging_t_kernel(tc, x, centers, out):
         def rows_of(i):
             return c_rows[:] if i == CENTRES else x_all[:, i, :, :]
 
+        def pair_of(i):
+            return (i + 1) // 2, ((i + 1) % 2) * PACK
+
         def sum_squares(i):
-            sumsq = work.tile([P, PACK], F32)
+            pair, col = pair_of(i)
+            if col == 0:
+                sumsq = norms.tile([P, 2 * PACK], F32)
+                st[("sumsq", pair)] = sumsq
+            sumsq = st[("sumsq", pair)]
             for j in range(PACK):
                 junk = work.tile([P, D], BF16)
                 nc.scalar.activation(
                     out=junk[:],
                     in_=rows_of(i)[:, j, :],
                     func=ACT.Square,
-                    accum_out=sumsq[:, j : j + 1],
+                    accum_out=sumsq[:, col + j : col + j + 1],
                 )
-            st[("sumsq", i)] = sumsq
-
-        def inverse_norm(i):
-            clamped = work.tile([P, PACK], F32)
-            nc.gpsimd.tensor_scalar_max(out=clamped[:], in0=st[("sumsq", i)][:], scalar1=EPS**4)
-            inv = work.tile([P, PACK], F32)
-            nc.gpsimd.tensor_tensor(out=inv[:], in0=clamped[:], in1=neg_half[:], op=ALU.pow)
-            st[("inv", i)] = inv
+            if col == PACK or i == NB - 1:
+                width = col + PACK
+                clamped = norms.tile([P, 2 * PACK], F32)
+                nc.gpsimd.tensor_scalar_max(
+                    out=clamped[:, :width], in0=sumsq[:, :width], scalar1=EPS**4
+                )
+                inv = norms.tile([P, 2 * PACK], F32)
+                nc.gpsimd.tensor_tensor(
+                    out=inv[:, :width], in0=clamped[:, :width], in1=neg_half[:, :width], op=ALU.pow
+                )
+                st[("inv", pair)] = inv
 
         def scale_rows(i, part):
-            inv = st[("inv", i)]
+            pair, col = pair_of(i)
+            inv = st[("inv", pair)][:, col : col + PACK]
             if part == 0:
                 unit = work.tile([P, PACK, D], BF16)
                 st[("unit", i)] = unit
@@ -305,43 +317,42 @@ def tile_token_merging_t_kernel(tc, x, centers, out):
             return 0 <= i < NB
 
         early = {-1: [0], 0: [1], 1: [2, 3], 2: [4, 5]}
-        for it in range(CENTRES, NB + 5):
+        for it in range(CENTRES, NB + 7):
             x_now = early.get(it, [it + X_LEAD] if it + X_LEAD < NB else [])
-            if real(it - 6) and (it - 6) % NBLK == NBLK - 1:
-                finish((it - 6) // NBLK)
-            if real(it - 4):
-                exponentials(it - 4)
-            if prep(it - 2):
-                turn(it - 2)
-            if prep(it - 3):
-                quantise_unit(it - 3)
+            if real(it - 8) and (it - 8) % NBLK == NBLK - 1:
+                finish((it - 8) // NBLK)
+            if real(it - 6):
+                exponentials(it - 6)
+            if prep(it - 4):
+                turn(it - 4)
+            if prep(it - 5):
+                quantise_unit(it - 5)
             for i in x_now:
                 regroup_x(i)
-            if prep(it - 2):
-                regroup_turned(it - 2)
+            if prep(it - 4):
+                regroup_turned(it - 4)
+            if real(it - 7):
+                add_probabilities(it - 7)
+            if real(it - 6):
+                inverse_sums(it - 6)
+            if prep(it - 3):
+                scale_rows(it - 3, 0)
+            if real(it - 6):
+                probabilities(it - 6)
+            if prep(it - 3):
+                scale_rows(it - 3, 1)
+            if real(it - 6):
+                regroup_prob(it - 6)
             if real(it - 5):
-                add_probabilities(it - 5)
-            if real(it - 4):
-                inverse_sums(it - 4)
-            if prep(it - 1):
-                scale_rows(it - 1, 0)
-            if real(it - 4):
-                probabilities(it - 4)
-            if prep(it - 1):
-                scale_rows(it - 1, 1)
-            if real(it - 4):
-                regroup_prob(it - 4)
-            if real(it - 3):
-                cosines(it - 3)
+                cosines(it - 5)
             for i in x_now:
                 quantise_x(i)
-            if real(it - 4):
-                quantise_prob(it - 4)
+            if real(it - 6):
+                quantise_prob(it - 6)
             if prep(it):
                 sum_squares(it)
-                inverse_norm(it)
+            if real(it - 7):
+                merge(it - 7)
             if real(it - 5):
-                merge(it - 5)
-            if real(it - 3):
-                row_max(it - 3)
+                row_max(it - 5)
         finish(B - 1)

@@ -22,8 +22,8 @@ EPS = 1e-8
 FLOPS = 2 * 2 * B * N * D * K
 
 CENTRES = -1
-VECTOR_COPY_EVERY = 6
-VECTOR_COPY_LATE = 26
+VECTOR_COPY_EVERY = 8
+VECTOR_COPY_LATE = (25, 27)
 X_LEAD = 3
 X_BUFS = X_LEAD + 9
 
@@ -123,7 +123,9 @@ def tile_token_merging_t_kernel(tc, x, centers, out):
         def regroup_turned(i):
             grouped = work.tile([P, PACK, P, PACK], BF16, align_bytes=64)
             for h in range(2):
-                if i >= VECTOR_COPY_LATE:
+                if i > VECTOR_COPY_LATE[1]:
+                    on_vector = False
+                elif i >= VECTOR_COPY_LATE[0]:
                     on_vector = h == 1
                 else:
                     on_vector = (2 * i + h) % VECTOR_COPY_EVERY == 1
@@ -233,7 +235,8 @@ def tile_token_merging_t_kernel(tc, x, centers, out):
         def regroup_prob(i):
             p_grouped = work.tile([P, K, PACK], BF16, align_bytes=64)
             nc.vector.tensor_copy(
-                out=p_grouped[:], in_=st[("prob", i)][:].rearrange("p j k -> p k j")
+                out=p_grouped[:].rearrange("p (c i) j -> p c j i", i=4),
+                in_=st[("prob", i)][:].rearrange("p j (c i) -> p c j i", i=4),
             )
             st[("pg", i)] = p_grouped
 

@@ -324,6 +324,8 @@ def tile_token_merging_t_kernel(tc, x, centers, out):
             x_now = early.get(it, [it + X_LEAD] if it + X_LEAD < NB else [])
             if real(it - 8) and (it - 8) % NBLK == NBLK - 1:
                 finish((it - 8) // NBLK)
+            if prep(it):
+                sum_squares(it)
             if real(it - 6):
                 exponentials(it - 6)
             if prep(it - 4):
@@ -352,8 +354,6 @@ def tile_token_merging_t_kernel(tc, x, centers, out):
                 quantise_x(i)
             if real(it - 6):
                 quantise_prob(it - 6)
-            if prep(it):
-                sum_squares(it)
             if real(it - 7):
                 merge(it - 7)
             if real(it - 5):

from contextlib import ExitStack

import concourse.mybir as mybir
from concourse.masks import make_identity

FP8X4 = mybir.dt.float8_e4m3fn_x4
BF16 = mybir.dt.bfloat16
F32 = mybir.dt.float32
U32 = mybir.dt.uint32
U8 = mybir.dt.uint8
ALU = mybir.AluOpType
ACT = mybir.ActivationFunctionType
AX = mybir.AxisListType

P = 128
PACK = 4
B, N, D, K = 2, 8192, 512, 256
BLOCK = P * PACK
NBLK = N // BLOCK
NB = B * NBLK
EPS = 1e-8
FLOPS = 2 * 2 * B * N * D * K

CENTRES = -1
VECTOR_COPY_EVERY = 8
VECTOR_COPY_LATE = (25, 27)
X_LEAD = 3
X_BUFS = X_LEAD + 9


def tile_token_merging_t_kernel(tc, x, centers, out):
    nc = tc.nc
    with ExitStack() as ctx:
        keep = ctx.enter_context(tc.tile_pool(name="keep", bufs=1))
        work = ctx.enter_context(tc.tile_pool(name="work", bufs=2))
        norms = ctx.enter_context(tc.tile_pool(name="norms", bufs=4))
        xq_pool = ctx.enter_context(tc.tile_pool(name="xq", bufs=X_BUFS))
        turn_pool = ctx.enter_context(tc.psum_pool(name="turn", bufs=2))
        cos_pool = ctx.enter_context(tc.psum_pool(name="cosp", bufs=2))
        acc_pool = ctx.enter_context(tc.psum_pool(name="acc", bufs=1))
        ctx.enter_context(tc.manual_schedule())

        ident = keep.tile([P, P], BF16)
        make_identity(nc, ident[:])
        ident_f = keep.tile([P, P], F32)
        make_identity(nc, ident_f[:])
        neg_half = keep.tile([P, 2 * PACK], F32)
        nc.vector.memset(neg_half[:], -0.5)

        c_rows = keep.tile([P, PACK, D], BF16)
        c_view = centers.rearrange("b (a p) d -> p (b a) d", p=P)
        for j in range(PACK):
            nc.sync.dma_start(out=c_rows[:, j, :], in_=c_view[:, j, :])
        x_all = keep.tile([P, NB, PACK, D], BF16)
        x_blocks = x.rearrange("b (g p j) d -> (b g) p j d", p=P, j=PACK)
        for i in range(NB):
            nc.sync.dma_start(out=x_all[:, i, :, :], in_=x_blocks[i])

        c_codes = keep.tile([P, B * K], U32, align_bytes=64)
        c_scales = keep.tile([P, B * K], U8, align_bytes=64)

        st = {}

        def rows_of(i):
            return c_rows[:] if i == CENTRES else x_all[:, i, :, :]

        def pair_of(i):
            return (i + 1) // 2, ((i + 1) % 2) * PACK

        def sum_squares(i):
            pair, col = pair_of(i)
            if col == 0:
                sumsq = norms.tile([P, 2 * PACK], F32)
                st[("sumsq", pair)] = sumsq
            sumsq = st[("sumsq", pair)]
            for j in range(PACK):
                junk = work.tile([P, D], BF16)
                nc.scalar.activation(
                    out=junk[:],
                    in_=rows_of(i)[:, j, :],
                    func=ACT.Square,
                    accum_out=sumsq[:, col + j : col + j + 1],
                )
            if col == PACK or i == NB - 1:
                width = col + PACK
                clamped = norms.tile([P, 2 * PACK], F32)
                nc.gpsimd.tensor_scalar_max(
                    out=clamped[:, :width], in0=sumsq[:, :width], scalar1=EPS**4
                )
                inv = norms.tile([P, 2 * PACK], F32)
                nc.gpsimd.tensor_tensor(
                    out=inv[:, :width], in0=clamped[:, :width], in1=neg_half[:, :width], op=ALU.pow
                )
                st[("inv", pair)] = inv

        def scale_rows(i, part):
            pair, col = pair_of(i)
            inv = st[("inv", pair)][:, col : col + PACK]
            if part == 0:
                unit = work.tile([P, PACK, D], BF16)
                st[("unit", i)] = unit
            unit = st[("unit", i)]
            for j in (2 * part, 2 * part + 1):
                nc.vector.tensor_scalar(
                    out=unit[:, j, :],
                    in0=rows_of(i)[:, j, :],
                    scalar1=inv[:, j : j + 1],
                    scalar2=None,
                    op0=ALU.mult,
                )

        def turn(i):
            unit = st[("unit", i)]
            for h in range(2):
                turned = turn_pool.tile([P, 2, PACK, P], BF16)
                for a in range(2):
                    for t in range(PACK):
                        nc.tensor.transpose(
                            turned[:, a, t, :], unit[:, 2 * h + a, t * P : (t + 1) * P], ident[:]
                        )
                st[("turned", i, h)] = turned

        def regroup_turned(i):
            grouped = work.tile([P, PACK, P, PACK], BF16, align_bytes=64)
            for h in range(2):
                if i > VECTOR_COPY_LATE[1]:
                    on_vector = False
                elif i >= VECTOR_COPY_LATE[0]:
                    on_vector = h == 1
                else:
                    on_vector = (2 * i + h) % VECTOR_COPY_EVERY == 1
                copier = nc.vector.tensor_copy if on_vector else nc.scalar.copy
                copier(
                    out=grouped[:, 2 * h : 2 * h + 2, :, :],
                    in_=st[("turned", i, h)][:].rearrange("p a t c -> p a c t"),
                )
            st[("grouped", i)] = grouped

        def quantise_unit(i):
            if i == CENTRES:
                codes, scales = c_codes, c_scales
            else:
                t_codes = work.tile([P, BLOCK], U32, align_bytes=64)
                t_scales = work.tile([P, BLOCK], U8, align_bytes=64)
                codes, scales = t_codes, t_scales
            nc.vector.quantize_mx(
                out=codes[:].bitcast(FP8X4),
                scales=scales[:],
                in_=st[("grouped", i)][:].rearrange("p j c t -> p (j c t)"),
            )
            st[("t", i)] = (codes, scales)

        def regroup_x(i):
            x_grouped = work.tile([P, D, PACK], BF16, align_bytes=64, bufs=3)
            nc.vector.tensor_copy(
                out=x_grouped[:].rearrange("p (c i) t -> p c t i", i=4),
                in_=rows_of(i).rearrange("p t (c i) -> p c t i", i=4),
            )
            st[("xg", i)] = x_grouped

        def quantise_x(i):
            x_codes = xq_pool.tile([P, D], U32, align_bytes=64)
            x_scales = xq_pool.tile([P, D], U8, align_bytes=64)
            nc.vector.quantize_mx(
                out=x_codes[:].bitcast(FP8X4),
                scales=x_scales[:],
                in_=st[("xg", i)][:].rearrange("p c t -> p (c t)"),
            )
            st[("x", i)] = (x_codes, x_scales)

        def cosines(i):
            b = i // NBLK
            codes, scales = st[("t", i)]
            for h in range(2):
                cos = cos_pool.tile([P, 2, K], F32)
                for a in range(2):
                    j = 2 * h + a
                    nc.tensor.matmul_mx(
                        out=cos[:, a, :],
                        lhsT=codes[:, j * P : (j + 1) * P].bitcast(FP8X4),
                        lhsT_scale=scales[:, j * P : (j + 1) * P],
                        rhs=c_codes[:, b * K : (b + 1) * K].bitcast(FP8X4),
                        rhs_scale=c_scales[:, b * K : (b + 1) * K],
                        start=True,
                        stop=True,
                    )
                st[("cos", i, h)] = cos

        def row_max(i):
            negmax = work.tile([P, PACK], F32)
            for h in range(2):
                nc.vector.tensor_reduce(
                    out=negmax[:, 2 * h : 2 * h + 2],
                    in_=st[("cos", i, h)][:],
                    axis=AX.X,
                    op=ALU.max,
                    negate=True,
                )
            st[("negmax", i)] = negmax

        def exponentials(i):
            negmax = st[("negmax", i)]
            esum = work.tile([P, PACK], F32)
            e = work.tile([P, PACK, K], F32)
            for j in range(PACK):
                nc.scalar.activation(
                    out=e[:, j, :],
                    in_=st[("cos", i, j // 2)][:, j % 2, :],
                    func=ACT.Exp,
                    bias=negmax[:, j : j + 1],
                    scale=1.0,
                    accum_out=esum[:, j : j + 1],
                )
            st[("e", i)] = (e, esum)

        def inverse_sums(i):
            rsum = work.tile([P, PACK], F32)
            nc.vector.reciprocal(out=rsum[:], in_=st[("e", i)][1][:])
            st[("rsum", i)] = rsum

        def probabilities(i):
            e = st[("e", i)][0]
            rsum = st[("rsum", i)]
            prob = work.tile([P, PACK, K], F32)
            for j in range(PACK):
                nc.vector.tensor_scalar(
                    out=prob[:, j, :],
                    in0=e[:, j, :],
                    scalar1=rsum[:, j : j + 1],
                    scalar2=None,
                    op0=ALU.mult,
                )
            st[("prob", i)] = prob

        def regroup_prob(i):
            p_grouped = work.tile([P, K, PACK], BF16, align_bytes=64)
            nc.vector.tensor_copy(
                out=p_grouped[:].rearrange("p (c i) j -> p c j i", i=4),
                in_=st[("prob", i)][:].rearrange("p j (c i) -> p c j i", i=4),
            )
            st[("pg", i)] = p_grouped

        def quantise_prob(i):
            p_codes = work.tile([P, K], U32, align_bytes=64)
            p_scales = work.tile([P, K], U8, align_bytes=64)
            nc.vector.quantize_mx(
                out=p_codes[:].bitcast(FP8X4),
                scales=p_scales[:],
                in_=st[("pg", i)][:].rearrange("p k j -> p (k j)"),
            )
            st[("p", i)] = (p_codes, p_scales)

        def add_probabilities(i):
            b, g = i // NBLK, i % NBLK
            if g == 0:
                sum0 = acc_pool.tile([P, P], F32)
                sum1 = acc_pool.tile([P, P], F32)
                st[("sum", b)] = [sum0, sum1]
            prob = st[("prob", i)]
            for h in range(2):
                for j in range(PACK):
                    nc.tensor.matmul(
                        out=st[("sum", b)][h][:],
                        lhsT=prob[:, j, h * P : (h + 1) * P],
                        rhs=ident_f[:],
                        is_transpose=True,
                        start=(g == 0 and j == 0),
                        stop=(g == NBLK - 1 and j == PACK - 1),
                    )

        def merge(i):
            b, g = i // NBLK, i % NBLK
            if g == 0:
                num0 = acc_pool.tile([P, D], F32)
                num1 = acc_pool.tile([P, D], F32)
                st[("num", b)] = [num0, num1]
            p_codes, p_scales = st[("p", i)][0], st[("p", i)][1]
            x_codes, x_scales = st[("x", i)]
            for h in range(2):
                nc.tensor.matmul_mx(
                    out=st[("num", b)][h][:],
                    lhsT=p_codes[:, h * P : (h + 1) * P].bitcast(FP8X4),
                    lhsT_scale=p_scales[:, h * P : (h + 1) * P],
                    rhs=x_codes[:].bitcast(FP8X4),
                    rhs_scale=x_scales[:],
                    start=(g == 0),
                    stop=(g == NBLK - 1),
                )

        def finish(b):
            den = work.tile([P, 2], F32)
            for h in range(2):
                nc.vector.tensor_reduce(
                    out=den[:, h : h + 1], in_=st[("sum", b)][h][:], axis=AX.X, op=ALU.add
                )
            den_eps = work.tile([P, 2], F32)
            nc.vector.tensor_scalar_add(out=den_eps[:], in0=den[:], scalar1=EPS)
            rden = work.tile([P, 2], F32)
            nc.vector.reciprocal(out=rden[:], in_=den_eps[:])
            for h in range(2):
                merged = work.tile([P, D], F32)
                if h == 0:
                    nc.scalar.activation(
                        out=merged[:], in_=st[("num", b)][h][:], func=ACT.Copy, scale=rden[:, h : h + 1]
                    )
                else:
                    nc.vector.tensor_scalar(
                        out=merged[:],
                        in0=st[("num", b)][h][:],
                        scalar1=rden[:, h : h + 1],
                        scalar2=None,
                        op0=ALU.mult,
                    )
                nc.sync.dma_start(out=out[b, h * P : (h + 1) * P, :], in_=merged[:])

        def prep(i):
            return CENTRES <= i < NB

        def real(i):
            return 0 <= i < NB

        early = {-1: [0], 0: [1], 1: [2, 3], 2: [4, 5]}
        for it in range(CENTRES, NB + 7):
            x_now = early.get(it, [it + X_LEAD] if it + X_LEAD < NB else [])
            if real(it - 8) and (it - 8) % NBLK == NBLK - 1:
                finish((it - 8) // NBLK)
            if prep(it):
                sum_squares(it)
            if real(it - 6):
                exponentials(it - 6)
            if prep(it - 4):
                turn(it - 4)
            if prep(it - 5):
                quantise_unit(it - 5)
            for i in x_now:
                regroup_x(i)
            if prep(it - 4):
                regroup_turned(it - 4)
            if real(it - 7):
                add_probabilities(it - 7)
            if real(it - 6):
                inverse_sums(it - 6)
            if prep(it - 3):
                scale_rows(it - 3, 0)
            if real(it - 6):
                probabilities(it - 6)
            if prep(it - 3):
                scale_rows(it - 3, 1)
            if real(it - 6):
                regroup_prob(it - 6)
            if real(it - 5):
                cosines(it - 5)
            for i in x_now:
                quantise_x(i)
            if real(it - 6):
                quantise_prob(it - 6)
            if real(it - 7):
                merge(it - 7)
            if real(it - 5):
                row_max(it - 5)
        finish(B - 1)
